import numpy as np
import ml_dtypes


def mxq(x, axis, fmt="e4m3"):
    dtype, down = {"e4m3": (ml_dtypes.float8_e4m3fn, 7), "e5m2": (ml_dtypes.float8_e5m2, 14)}[fmt]
    v = np.moveaxis(np.asarray(x, np.float32).astype(ml_dtypes.bfloat16).astype(np.float64), axis, -1)
    blocks = v.reshape(v.shape[:-1] + (-1, 32))
    amax = np.abs(blocks).max(-1, keepdims=True)
    byte = np.maximum(np.where(amax > 0, np.frexp(amax)[1] - 1 + 127, 0) - down, 1)
    scale = np.exp2(byte - 127.0)
    codes = (blocks / scale).astype(np.float32).astype(dtype).astype(np.float64)
    return np.moveaxis((codes * scale).reshape(v.shape), -1, axis)


WIDE = False


def mx_kscale(k):
    if not WIDE:
        return np.ones(k)
    levels = np.array([10, -10, 5, -5, 0])
    a = np.random.permutation(np.resize(levels, k // 512 * 4)).reshape(k // 512, 4)
    idx = np.arange(k)
    return np.exp2(a[idx // 512, idx % 128 // 32])


BF16 = ml_dtypes.bfloat16


def bf(x):
    return np.asarray(x, np.float32).astype(BF16)


def f64(x):
    return np.asarray(x).astype(np.float64)


B, D0, D1, D2, D3, D4 = 512, 1024, 2048, 2048, 1024, 256
DENSITY = 0.02


def setup_inputs():
    s, t = mx_kscale(D0), mx_kscale(D1)
    bound0 = np.sqrt(3.0 / (DENSITY * D0))
    bound1 = np.sqrt(6.0 / (DENSITY * D1))
    return {"x": bf(np.random.standard_normal((B, D0)) * s),
            "W0": bf(np.random.uniform(-bound0, bound0, (D1, D0)) / s[None, :] * t[:, None]),
            "b0": bf(np.random.standard_normal(D1) * 0.3 * t),
            "m0": bf(np.random.uniform(size=(D1, D0)) < DENSITY),
            "W1": bf(np.random.uniform(-bound1, bound1, (D2, D1)) / t[None, :]),
            "b1": bf(np.random.standard_normal(D2) * 0.3),
            "m1": bf(np.random.uniform(size=(D2, D1)) < DENSITY)}


def reference(x, W0, b0, m0, W1, b1, m1):
    h = f64(x).reshape(x.shape[0], -1)
    w0 = f64(W0) * f64(m0)
    pre0 = (mxq(h, 1, "e4m3") @ mxq(w0, 1, "e4m3").T) + f64(b0)
    h0 = np.maximum(pre0, 0.0)
    w1 = f64(W1) * f64(m1)
    pre1 = (mxq(h0, 1, "e4m3") @ mxq(w1, 1, "e4m3").T) + f64(b1)
    return np.maximum(pre1, 0.0)

@@ -1,0 +1,212 @@
+from contextlib import ExitStack
+
+import concourse.mybir as mybir
+from concourse.masks import make_identity
+
+F32 = mybir.dt.float32
+BF16 = mybir.dt.bfloat16
+U32 = mybir.dt.uint32
+U8 = mybir.dt.uint8
+FP8X4 = mybir.dt.float8_e4m3fn_x4
+MULT = mybir.AluOpType.mult
+ADD = mybir.AluOpType.add
+RELU = mybir.ActivationFunctionType.Relu
+
+P = 128
+PACK = 4
+K_PASS = P * PACK
+BANK = 512
+BATCH, D0, D1, D2 = 512, 1024, 2048, 2048
+PASSES0 = D0 // K_PASS
+PASSES1 = D1 // K_PASS
+BATCH_TILES = BATCH // P
+CHUNK = 4096
+ROWS1 = 256
+LAST_CHUNK = D2 // ROWS1 - 1
+
+FLOPS = 2 * BATCH * D0 * D1 + 2 * BATCH * D1 * D2
+
+
+def tile_patchedsparsenetwork_pa_kernel(tc, x, W0, b0, m0, W1, b1, m1, out):
+    nc = tc.nc
+    with ExitStack() as ctx:
+        const = ctx.enter_context(tc.tile_pool(name="const", bufs=1))
+        weights = ctx.enter_context(tc.tile_pool(name="weights", bufs=6))
+        stage = ctx.enter_context(tc.tile_pool(name="stage", bufs=3))
+        results = ctx.enter_context(tc.tile_pool(name="results", bufs=6))
+        tr_psum = ctx.enter_context(tc.psum_pool(name="tr_psum", bufs=4))
+        acc_psum = ctx.enter_context(tc.psum_pool(name="acc_psum", bufs=4))
+
+        x_rows = const.tile([P, BATCH_TILES * D0], BF16)
+        nc.sync.dma_start(out=x_rows[:], in_=x.rearrange("(q r) k -> q (r k)", r=BATCH_TILES))
+
+        b0_rows = const.tile([P, 2 * P], BF16)
+        b1_row = const.tile([P, D2], BF16)
+        ones = const.tile([P, P], BF16)
+        nc.vector.memset(b0_rows[:], 0.0)
+        nc.vector.memset(b1_row[:], 0.0)
+        nc.vector.memset(ones[:], 1.0)
+        nc.sync.dma_start(out=b0_rows[0 : D1 // 256, :], in_=b0.rearrange("(j c) -> j c", c=256))
+        nc.sync.dma_start(out=b1_row[0:1, :], in_=b1.rearrange("(o d) -> o d", o=1))
+
+        ident = const.tile([P, P], F32)
+        make_identity(nc, ident[:])
+
+        x_words = x_rows[:].bitcast(F32).rearrange("q (r w) -> q r w", r=BATCH_TILES)
+        x_grouped = const.tile([P, PASSES0 * BATCH * PACK], BF16, align_bytes=64)
+        x_grouped_words = x_grouped[:].bitcast(F32).rearrange(
+            "p (g r q u) -> p g r q u", g=PASSES0, r=BATCH_TILES, u=2
+        )
+        for g in range(PASSES0):
+            for half in range(2):
+                bank = tr_psum.tile([P, 2, 2, P], F32, tag="tr")
+                for rr in range(2):
+                    for u in range(2):
+                        first = 256 * g + P * u
+                        nc.tensor.transpose(
+                            bank[:, rr, u, :], x_words[:, 2 * half + rr, first : first + P], ident[:]
+                        )
+                nc.scalar.copy(
+                    out=x_grouped_words[:, g, 2 * half : 2 * half + 2, :, :],
+                    in_=bank[:].rearrange("p r u q -> p r q u"),
+                )
+        x_codes = const.tile([P, PASSES0 * BATCH], U32, align_bytes=64)
+        x_scales = const.tile([P, PASSES0 * BATCH], U8, align_bytes=64)
+        nc.vector.quantize_mx(out=x_codes[:].bitcast(FP8X4), scales=x_scales[:], in_=x_grouped[:])
+
+        b0_bank = tr_psum.tile([P, BANK], F32, tag="tr")
+        nc.tensor.transpose(b0_bank[:, 0:P], b0_rows[:].bitcast(F32), ident[:])
+        b0_cols = const.tile([P, D1 // P], F32)
+        nc.vector.tensor_copy(out=b0_cols[:], in_=b0_bank[:, 0 : D1 // 256].bitcast(BF16))
+
+        b1_all = const.tile([P, D2], F32)
+        for i in range(D2 // BANK):
+            cols = slice(BANK * i, BANK * (i + 1))
+            b1_bank = acc_psum.tile([P, BANK], F32, tag="acc")
+            nc.tensor.matmul(b1_bank[:], lhsT=ones[:], rhs=b1_row[:, cols], start=True, stop=True)
+            nc.scalar.copy(out=b1_all[:, cols], in_=b1_bank[:])
+
+        h_codes = const.tile([P, PASSES1 * BATCH], U32, align_bytes=64)
+        h_scales = const.tile([P, PASSES1 * BATCH], U8, align_bytes=64)
+
+        for g in range(PASSES1):
+            rows = slice(K_PASS * g, K_PASS * (g + 1))
+            w = weights.tile([P, CHUNK], BF16, tag="w")
+            m = weights.tile([P, CHUNK], BF16, tag="m")
+            nc.sync.dma_start(
+                out=w[:].rearrange("q (u c) -> q u c", u=2),
+                in_=W0[rows, :].rearrange("(u q e) k -> q u (e k)", u=2, e=2),
+            )
+            nc.sync.dma_start(
+                out=m[:].rearrange("q (u c) -> q u c", u=2),
+                in_=m0[rows, :].rearrange("(u q e) k -> q u (e k)", u=2, e=2),
+            )
+            nc.vector.tensor_tensor(out=w[:], in0=w[:], in1=m[:], op=MULT)
+
+            w_words = w[:].bitcast(F32)
+            grouped = stage.tile([P, CHUNK], BF16, tag="grouped", align_bytes=64)
+            grouped_words = grouped[:].bitcast(F32).rearrange(
+                "p (t g q u) -> p t g q u", t=PACK, g=PASSES0, u=2
+            )
+            for t in range(PACK):
+                bank = tr_psum.tile([P, 4, P], F32, tag="tr")
+                for s in range(4):
+                    first = (D0 // 2) * t + P * s
+                    nc.tensor.transpose(bank[:, s, :], w_words[:, first : first + P], ident[:])
+                nc.scalar.copy(
+                    out=grouped_words[:, t], in_=bank[:].rearrange("p (g u) q -> p g q u", u=2)
+                )
+            codes = stage.tile([P, CHUNK // PACK], U32, tag="codes", align_bytes=64)
+            scales = stage.tile([P, CHUNK // PACK], U8, tag="scales", align_bytes=64)
+            nc.vector.quantize_mx(out=codes[:].bitcast(FP8X4), scales=scales[:], in_=grouped[:])
+
+            h_rows = stage.tile([P, PACK, BATCH], BF16, tag="h_rows")
+            for t in range(PACK):
+                acc = acc_psum.tile([P, BATCH], F32, tag="acc")
+                for g0 in range(PASSES0):
+                    w_cols = slice(P * (PASSES0 * t + g0), P * (PASSES0 * t + g0 + 1))
+                    x_cols = slice(BATCH * g0, BATCH * (g0 + 1))
+                    nc.tensor.matmul_mx(
+                        out=acc[:],
+                        lhsT=codes[:, w_cols].bitcast(FP8X4),
+                        lhsT_scale=scales[:, w_cols],
+                        rhs=x_codes[:, x_cols].bitcast(FP8X4),
+                        rhs_scale=x_scales[:, x_cols],
+                        start=(g0 == 0),
+                        stop=(g0 == PASSES0 - 1),
+                    )
+                column = PACK * g + t
+                nc.scalar.activation(
+                    out=h_rows[:, t, :], in_=acc[:], func=RELU, bias=b0_cols[:, column : column + 1]
+                )
+            h_grouped = stage.tile([P, BATCH, PACK], BF16, tag="h_grouped", align_bytes=64)
+            nc.vector.tensor_copy(out=h_grouped[:], in_=h_rows[:].rearrange("p t n -> p n t"))
+            h_cols = slice(BATCH * g, BATCH * (g + 1))
+            nc.vector.quantize_mx(
+                out=h_codes[:, h_cols].bitcast(FP8X4),
+                scales=h_scales[:, h_cols],
+                in_=h_grouped[:].rearrange("p n t -> p (n t)"),
+            )
+
+        out_view = out.rearrange("(q r) d -> q r d", r=BATCH_TILES)
+        for c in range(D2 // ROWS1):
+            rows = slice(ROWS1 * c, ROWS1 * (c + 1))
+            w = weights.tile([P, CHUNK], BF16, tag="w")
+            m = weights.tile([P, CHUNK], BF16, tag="m")
+            nc.sync.dma_start(out=w[:], in_=W1[rows, :].rearrange("(q r) k -> q (r k)", r=2))
+            nc.sync.dma_start(out=m[:], in_=m1[rows, :].rearrange("(q r) k -> q (r k)", r=2))
+
+            pieces = PASSES1 if c == LAST_CHUNK else 1
+            w_rows = w[:].rearrange("q (r k) -> q r k", r=2)
+            m_rows = m[:].rearrange("q (r k) -> q r k", r=2)
+            w_words = w[:].bitcast(F32).rearrange("q (r w) -> q r w", r=2)
+            grouped = stage.tile([P, CHUNK], BF16, tag="grouped", align_bytes=64)
+            grouped_words = grouped[:].bitcast(F32).rearrange(
+                "p (g q s) -> p g q s", g=PASSES1, s=4
+            )
+            codes = stage.tile([P, CHUNK // PACK], U32, tag="codes", align_bytes=64)
+            scales = stage.tile([P, CHUNK // PACK], U8, tag="scales", align_bytes=64)
+            for piece in range(pieces):
+                first_pass = piece * PASSES1 // pieces
+                end_pass = (piece + 1) * PASSES1 // pieces
+                k_cols = slice(K_PASS * first_pass, K_PASS * end_pass)
+                nc.vector.tensor_tensor(
+                    out=w_rows[:, :, k_cols], in0=w_rows[:, :, k_cols], in1=m_rows[:, :, k_cols], op=MULT
+                )
+                for g in range(first_pass, end_pass):
+                    bank = tr_psum.tile([P, 4, P], F32, tag="tr")
+                    for r in range(2):
+                        for u in range(2):
+                            first = 256 * g + P * u
+                            nc.tensor.transpose(
+                                bank[:, 2 * r + u, :], w_words[:, r, first : first + P], ident[:]
+                            )
+                    nc.scalar.copy(out=grouped_words[:, g], in_=bank[:].rearrange("p s q -> p q s"))
+                n_cols = slice(ROWS1 * first_pass, ROWS1 * end_pass)
+                nc.vector.quantize_mx(
+                    out=codes[:, n_cols].bitcast(FP8X4),
+                    scales=scales[:, n_cols],
+                    in_=grouped[:, PACK * ROWS1 * first_pass : PACK * ROWS1 * end_pass],
+                )
+
+            bias = b1_all[:, rows].unsqueeze(1).to_broadcast([P, 2, ROWS1])
+            for half in range(2):
+                acc = acc_psum.tile([P, 2, ROWS1], F32, tag="acc")
+                for rr in range(2):
+                    r = 2 * half + rr
+                    for g in range(PASSES1):
+                        h_cols = slice(BATCH * g + P * r, BATCH * g + P * (r + 1))
+                        w_cols = slice(ROWS1 * g, ROWS1 * (g + 1))
+                        nc.tensor.matmul_mx(
+                            out=acc[:, rr, :],
+                            lhsT=h_codes[:, h_cols].bitcast(FP8X4),
+                            lhsT_scale=h_scales[:, h_cols],
+                            rhs=codes[:, w_cols].bitcast(FP8X4),
+                            rhs_scale=scales[:, w_cols],
+                            start=(g == 0),
+                            stop=(g == PASSES1 - 1),
+                        )
+                result = results.tile([P, 2, ROWS1], F32, tag="result")
+                nc.vector.tensor_tensor(out=result[:], in0=acc[:], in1=bias, op=ADD)
+                nc.scalar.activation(out=result[:], in_=result[:], func=RELU)
+                nc.scalar.dma_start(out=out_view[:, 2 * half : 2 * half + 2, rows], in_=result[:])

@@ -20,9 +20,13 @@ BATCH, D0, D1, D2 = 512, 1024, 2048, 2048
 PASSES0 = D0 // K_PASS
 PASSES1 = D1 // K_PASS
 BATCH_TILES = BATCH // P
-CHUNK = 4096
-ROWS1 = 256
-LAST_CHUNK = D2 // ROWS1 - 1
+UNIT = 2048
+ROWS0 = P * UNIT // D0
+ROWS1 = P * UNIT // D1
+UNITS0 = D1 // ROWS0
+UNITS = UNITS0 + D2 // ROWS1
+AHEAD = 8
+STORE_COLS = 2 * ROWS1
 
 FLOPS = 2 * BATCH * D0 * D1 + 2 * BATCH * D1 * D2
 
@@ -30,15 +34,131 @@ FLOPS = 2 * BATCH * D0 * D1 + 2 * BATCH * D1 * D2
 def tile_patchedsparsenetwork_pa_kernel(tc, x, W0, b0, m0, W1, b1, m1, out):
     nc = tc.nc
     with ExitStack() as ctx:
+        ctx.enter_context(tc.manual_schedule())
         const = ctx.enter_context(tc.tile_pool(name="const", bufs=1))
-        weights = ctx.enter_context(tc.tile_pool(name="weights", bufs=6))
+        weights = ctx.enter_context(tc.tile_pool(name="weights", bufs=AHEAD + 2))
         stage = ctx.enter_context(tc.tile_pool(name="stage", bufs=3))
-        results = ctx.enter_context(tc.tile_pool(name="results", bufs=6))
         tr_psum = ctx.enter_context(tc.psum_pool(name="tr_psum", bufs=4))
         acc_psum = ctx.enter_context(tc.psum_pool(name="acc_psum", bufs=4))
 
+        w_of, m_of, grouped_of, codes_of, scales_of, acc_of = {}, {}, {}, {}, {}, {}
+        h_rows_of, result_of = {}, {}
+
+        def load(i):
+            w = weights.tile([P, UNIT], BF16, tag="w")
+            m = weights.tile([P, UNIT], BF16, tag="m")
+            if i < UNITS0:
+                rows = slice(ROWS0 * i, ROWS0 * (i + 1))
+                nc.sync.dma_start(out=w[:], in_=W0[rows, :].rearrange("(q e) k -> q (e k)", e=2))
+                nc.sync.dma_start(out=m[:], in_=m0[rows, :].rearrange("(q e) k -> q (e k)", e=2))
+            else:
+                rows = slice(ROWS1 * (i - UNITS0), ROWS1 * (i - UNITS0 + 1))
+                nc.sync.dma_start(out=w[:], in_=W1[rows, :])
+                nc.sync.dma_start(out=m[:], in_=m1[rows, :])
+            w_of[i], m_of[i] = w, m
+
+        def multiply(i):
+            nc.vector.tensor_tensor(out=w_of[i][:], in0=w_of[i][:], in1=m_of[i][:], op=MULT)
+
+        def transpose(i):
+            w_words = w_of[i][:].bitcast(F32)
+            grouped = stage.tile([P, UNIT], BF16, tag="grouped", align_bytes=64)
+            grouped_words = grouped[:].bitcast(F32).rearrange(
+                "p (a c q u) -> p a c q u", a=2, c=2, u=2
+            )
+            for a in range(2):
+                bank = tr_psum.tile([P, 4, P], F32, tag="tr")
+                for s in range(4):
+                    first = P * (4 * a + s)
+                    nc.tensor.transpose(bank[:, s, :], w_words[:, first : first + P], ident[:])
+                nc.scalar.copy(
+                    out=grouped_words[:, a], in_=bank[:].rearrange("p (c u) q -> p c q u", u=2)
+                )
+            grouped_of[i] = grouped
+
+        def quantise(i):
+            codes = stage.tile([P, UNIT // PACK], U32, tag="codes", align_bytes=64)
+            scales = stage.tile([P, UNIT // PACK], U8, tag="scales", align_bytes=64)
+            nc.vector.quantize_mx(
+                out=codes[:].bitcast(FP8X4), scales=scales[:], in_=grouped_of[i][:]
+            )
+            codes_of[i], scales_of[i] = codes, scales
+
+        def layer0_matmuls(j):
+            g, u = divmod(j, 2)
+            if u == 0:
+                h_rows = stage.tile([P, PACK, BATCH], BF16, tag="h_rows")
+                h_rows_of[g] = h_rows
+            for e in range(2):
+                acc = acc_psum.tile([P, BATCH], F32, tag="acc")
+                for g0 in range(PASSES0):
+                    w_cols = slice(P * (PASSES0 * e + g0), P * (PASSES0 * e + g0 + 1))
+                    x_cols = slice(BATCH * g0, BATCH * (g0 + 1))
+                    nc.tensor.matmul_mx(
+                        out=acc[:],
+                        lhsT=codes_of[j][:, w_cols].bitcast(FP8X4),
+                        lhsT_scale=scales_of[j][:, w_cols],
+                        rhs=x_codes[:, x_cols].bitcast(FP8X4),
+                        rhs_scale=x_scales[:, x_cols],
+                        start=(g0 == 0),
+                        stop=(g0 == PASSES0 - 1),
+                    )
+                nc.scalar.activation(
+                    out=h_rows_of[g][:, 2 * u + e, :],
+                    in_=acc[:],
+                    func=RELU,
+                    bias=b0_cols[:, 2 * j + e : 2 * j + e + 1],
+                )
+
+        def layer0_finish(j):
+            g, u = divmod(j, 2)
+            if u == 1:
+                h_grouped = stage.tile([P, BATCH, PACK], BF16, tag="h_grouped", align_bytes=64)
+                nc.vector.tensor_copy(
+                    out=h_grouped[:], in_=h_rows_of[g][:].rearrange("p t n -> p n t")
+                )
+                h_cols = slice(BATCH * g, BATCH * (g + 1))
+                nc.vector.quantize_mx(
+                    out=h_codes[:, h_cols].bitcast(FP8X4),
+                    scales=h_scales[:, h_cols],
+                    in_=h_grouped[:].rearrange("p n t -> p (n t)"),
+                )
+
+        def layer1_matmuls(k):
+            acc = acc_psum.tile([P, BATCH_TILES, ROWS1], F32, tag="acc")
+            for r in range(BATCH_TILES):
+                for g in range(PASSES1):
+                    h_cols = slice(BATCH * g + P * r, BATCH * g + P * (r + 1))
+                    w_cols = slice(ROWS1 * g, ROWS1 * (g + 1))
+                    nc.tensor.matmul_mx(
+                        out=acc[:, r, :],
+                        lhsT=h_codes[:, h_cols].bitcast(FP8X4),
+                        lhsT_scale=h_scales[:, h_cols],
+                        rhs=codes_of[UNITS0 + k][:, w_cols].bitcast(FP8X4),
+                        rhs_scale=scales_of[UNITS0 + k][:, w_cols],
+                        start=(g == 0),
+                        stop=(g == PASSES1 - 1),
+                    )
+            acc_of[k] = acc
+
+        def layer1_finish(k):
+            store, a = divmod(k, 2)
+            if a == 0:
+                result = stage.tile([P, BATCH_TILES, STORE_COLS], F32, tag="result")
+                result_of[store] = result
+            part = result_of[store][:, :, ROWS1 * a : ROWS1 * (a + 1)]
+            bias = b1_all[:, ROWS1 * k : ROWS1 * (k + 1)].unsqueeze(1)
+            nc.vector.tensor_tensor(
+                out=part, in0=acc_of[k][:], in1=bias.to_broadcast([P, BATCH_TILES, ROWS1]), op=ADD
+            )
+            nc.scalar.activation(out=part, in_=part, func=RELU)
+            if a == 1:
+                cols = slice(STORE_COLS * store, STORE_COLS * (store + 1))
+                nc.scalar.dma_start(out=out_view[:, :, cols], in_=result_of[store][:])
+
         x_rows = const.tile([P, BATCH_TILES * D0], BF16)
         nc.sync.dma_start(out=x_rows[:], in_=x.rearrange("(q r) k -> q (r k)", r=BATCH_TILES))
+        out_view = out.rearrange("(q r) d -> q r d", r=BATCH_TILES)
 
         b0_rows = const.tile([P, 2 * P], BF16)
         b1_row = const.tile([P, D2], BF16)
@@ -48,6 +168,8 @@ def tile_patchedsparsenetwork_pa_kernel(tc, x, W0, b0, m0, W1, b1, m1, out):
         nc.vector.memset(ones[:], 1.0)
         nc.sync.dma_start(out=b0_rows[0 : D1 // 256, :], in_=b0.rearrange("(j c) -> j c", c=256))
         nc.sync.dma_start(out=b1_row[0:1, :], in_=b1.rearrange("(o d) -> o d", o=1))
+        for i in range(AHEAD):
+            load(i)
 
         ident = const.tile([P, P], F32)
         make_identity(nc, ident[:])
@@ -57,19 +179,14 @@ def tile_patchedsparsenetwork_pa_kernel(tc, x, W0, b0, m0, W1, b1, m1, out):
         x_grouped_words = x_grouped[:].bitcast(F32).rearrange(
             "p (g r q u) -> p g r q u", g=PASSES0, r=BATCH_TILES, u=2
         )
-        for g in range(PASSES0):
-            for half in range(2):
-                bank = tr_psum.tile([P, 2, 2, P], F32, tag="tr")
-                for rr in range(2):
-                    for u in range(2):
-                        first = 256 * g + P * u
-                        nc.tensor.transpose(
-                            bank[:, rr, u, :], x_words[:, 2 * half + rr, first : first + P], ident[:]
-                        )
-                nc.scalar.copy(
-                    out=x_grouped_words[:, g, 2 * half : 2 * half + 2, :, :],
-                    in_=bank[:].rearrange("p r u q -> p r q u"),
-                )
+        for r in range(BATCH_TILES):
+            bank = tr_psum.tile([P, 4, P], F32, tag="tr")
+            for s in range(4):
+                nc.tensor.transpose(bank[:, s, :], x_words[:, r, P * s : P * (s + 1)], ident[:])
+            nc.scalar.copy(
+                out=x_grouped_words[:, :, r, :, :],
+                in_=bank[:].rearrange("p (g u) q -> p g q u", u=2),
+            )
         x_codes = const.tile([P, PASSES0 * BATCH], U32, align_bytes=64)
         x_scales = const.tile([P, PASSES0 * BATCH], U8, align_bytes=64)
         nc.vector.quantize_mx(out=x_codes[:].bitcast(FP8X4), scales=x_scales[:], in_=x_grouped[:])
@@ -89,124 +206,20 @@ def tile_patchedsparsenetwork_pa_kernel(tc, x, W0, b0, m0, W1, b1, m1, out):
         h_codes = const.tile([P, PASSES1 * BATCH], U32, align_bytes=64)
         h_scales = const.tile([P, PASSES1 * BATCH], U8, align_bytes=64)
 
-        for g in range(PASSES1):
-            rows = slice(K_PASS * g, K_PASS * (g + 1))
-            w = weights.tile([P, CHUNK], BF16, tag="w")
-            m = weights.tile([P, CHUNK], BF16, tag="m")
-            nc.sync.dma_start(
-                out=w[:].rearrange("q (u c) -> q u c", u=2),
-                in_=W0[rows, :].rearrange("(u q e) k -> q u (e k)", u=2, e=2),
-            )
-            nc.sync.dma_start(
-                out=m[:].rearrange("q (u c) -> q u c", u=2),
-                in_=m0[rows, :].rearrange("(u q e) k -> q u (e k)", u=2, e=2),
-            )
-            nc.vector.tensor_tensor(out=w[:], in0=w[:], in1=m[:], op=MULT)
-
-            w_words = w[:].bitcast(F32)
-            grouped = stage.tile([P, CHUNK], BF16, tag="grouped", align_bytes=64)
-            grouped_words = grouped[:].bitcast(F32).rearrange(
-                "p (t g q u) -> p t g q u", t=PACK, g=PASSES0, u=2
-            )
-            for t in range(PACK):
-                bank = tr_psum.tile([P, 4, P], F32, tag="tr")
-                for s in range(4):
-                    first = (D0 // 2) * t + P * s
-                    nc.tensor.transpose(bank[:, s, :], w_words[:, first : first + P], ident[:])
-                nc.scalar.copy(
-                    out=grouped_words[:, t], in_=bank[:].rearrange("p (g u) q -> p g q u", u=2)
-                )
-            codes = stage.tile([P, CHUNK // PACK], U32, tag="codes", align_bytes=64)
-            scales = stage.tile([P, CHUNK // PACK], U8, tag="scales", align_bytes=64)
-            nc.vector.quantize_mx(out=codes[:].bitcast(FP8X4), scales=scales[:], in_=grouped[:])
-
-            h_rows = stage.tile([P, PACK, BATCH], BF16, tag="h_rows")
-            for t in range(PACK):
-                acc = acc_psum.tile([P, BATCH], F32, tag="acc")
-                for g0 in range(PASSES0):
-                    w_cols = slice(P * (PASSES0 * t + g0), P * (PASSES0 * t + g0 + 1))
-                    x_cols = slice(BATCH * g0, BATCH * (g0 + 1))
-                    nc.tensor.matmul_mx(
-                        out=acc[:],
-                        lhsT=codes[:, w_cols].bitcast(FP8X4),
-                        lhsT_scale=scales[:, w_cols],
-                        rhs=x_codes[:, x_cols].bitcast(FP8X4),
-                        rhs_scale=x_scales[:, x_cols],
-                        start=(g0 == 0),
-                        stop=(g0 == PASSES0 - 1),
-                    )
-                column = PACK * g + t
-                nc.scalar.activation(
-                    out=h_rows[:, t, :], in_=acc[:], func=RELU, bias=b0_cols[:, column : column + 1]
-                )
-            h_grouped = stage.tile([P, BATCH, PACK], BF16, tag="h_grouped", align_bytes=64)
-            nc.vector.tensor_copy(out=h_grouped[:], in_=h_rows[:].rearrange("p t n -> p n t"))
-            h_cols = slice(BATCH * g, BATCH * (g + 1))
-            nc.vector.quantize_mx(
-                out=h_codes[:, h_cols].bitcast(FP8X4),
-                scales=h_scales[:, h_cols],
-                in_=h_grouped[:].rearrange("p n t -> p (n t)"),
-            )
-
-        out_view = out.rearrange("(q r) d -> q r d", r=BATCH_TILES)
-        for c in range(D2 // ROWS1):
-            rows = slice(ROWS1 * c, ROWS1 * (c + 1))
-            w = weights.tile([P, CHUNK], BF16, tag="w")
-            m = weights.tile([P, CHUNK], BF16, tag="m")
-            nc.sync.dma_start(out=w[:], in_=W1[rows, :].rearrange("(q r) k -> q (r k)", r=2))
-            nc.sync.dma_start(out=m[:], in_=m1[rows, :].rearrange("(q r) k -> q (r k)", r=2))
-
-            pieces = PASSES1 if c == LAST_CHUNK else 1
-            w_rows = w[:].rearrange("q (r k) -> q r k", r=2)
-            m_rows = m[:].rearrange("q (r k) -> q r k", r=2)
-            w_words = w[:].bitcast(F32).rearrange("q (r w) -> q r w", r=2)
-            grouped = stage.tile([P, CHUNK], BF16, tag="grouped", align_bytes=64)
-            grouped_words = grouped[:].bitcast(F32).rearrange(
-                "p (g q s) -> p g q s", g=PASSES1, s=4
-            )
-            codes = stage.tile([P, CHUNK // PACK], U32, tag="codes", align_bytes=64)
-            scales = stage.tile([P, CHUNK // PACK], U8, tag="scales", align_bytes=64)
-            for piece in range(pieces):
-                first_pass = piece * PASSES1 // pieces
-                end_pass = (piece + 1) * PASSES1 // pieces
-                k_cols = slice(K_PASS * first_pass, K_PASS * end_pass)
-                nc.vector.tensor_tensor(
-                    out=w_rows[:, :, k_cols], in0=w_rows[:, :, k_cols], in1=m_rows[:, :, k_cols], op=MULT
-                )
-                for g in range(first_pass, end_pass):
-                    bank = tr_psum.tile([P, 4, P], F32, tag="tr")
-                    for r in range(2):
-                        for u in range(2):
-                            first = 256 * g + P * u
-                            nc.tensor.transpose(
-                                bank[:, 2 * r + u, :], w_words[:, r, first : first + P], ident[:]
-                            )
-                    nc.scalar.copy(out=grouped_words[:, g], in_=bank[:].rearrange("p s q -> p q s"))
-                n_cols = slice(ROWS1 * first_pass, ROWS1 * end_pass)
-                nc.vector.quantize_mx(
-                    out=codes[:, n_cols].bitcast(FP8X4),
-                    scales=scales[:, n_cols],
-                    in_=grouped[:, PACK * ROWS1 * first_pass : PACK * ROWS1 * end_pass],
-                )
-
-            bias = b1_all[:, rows].unsqueeze(1).to_broadcast([P, 2, ROWS1])
-            for half in range(2):
-                acc = acc_psum.tile([P, 2, ROWS1], F32, tag="acc")
-                for rr in range(2):
-                    r = 2 * half + rr
-                    for g in range(PASSES1):
-                        h_cols = slice(BATCH * g + P * r, BATCH * g + P * (r + 1))
-                        w_cols = slice(ROWS1 * g, ROWS1 * (g + 1))
-                        nc.tensor.matmul_mx(
-                            out=acc[:, rr, :],
-                            lhsT=h_codes[:, h_cols].bitcast(FP8X4),
-                            lhsT_scale=h_scales[:, h_cols],
-                            rhs=codes[:, w_cols].bitcast(FP8X4),
-                            rhs_scale=scales[:, w_cols],
-                            start=(g == 0),
-                            stop=(g == PASSES1 - 1),
-                        )
-                result = results.tile([P, 2, ROWS1], F32, tag="result")
-                nc.vector.tensor_tensor(out=result[:], in0=acc[:], in1=bias, op=ADD)
-                nc.scalar.activation(out=result[:], in_=result[:], func=RELU)
-                nc.scalar.dma_start(out=out_view[:, 2 * half : 2 * half + 2, rows], in_=result[:])
+        for s in range(UNITS + 3):
+            if s + AHEAD < UNITS:
+                load(s + AHEAD)
+            if 0 <= s - 2 < UNITS:
+                quantise(s - 2)
+            if 0 <= s - 1 < UNITS:
+                transpose(s - 1)
+            if 0 <= s - 3 < UNITS0:
+                layer0_finish(s - 3)
+            if UNITS0 <= s - 3 < UNITS:
+                layer1_finish(s - 3 - UNITS0)
+            if 0 <= s - 2 < UNITS0:
+                layer0_matmuls(s - 2)
+            if UNITS0 <= s - 2 < UNITS:
+                layer1_matmuls(s - 2 - UNITS0)
+            if s < UNITS:
+                multiply(s)

@@ -25,8 +25,16 @@ ROWS0 = P * UNIT // D0
 ROWS1 = P * UNIT // D1
 UNITS0 = D1 // ROWS0
 UNITS = UNITS0 + D2 // ROWS1
-AHEAD = 8
+UNITS1 = D2 // ROWS1
 STORE_COLS = 2 * ROWS1
+
+LAG_TRANSPOSE = 1
+LAG_QUANTISE = 3
+LAG_MATMUL0 = 3
+LAG_FINISH0 = 5
+LAG_MATMUL1 = 4
+LAG_FINISH1 = 6
+AHEAD = 10
 
 FLOPS = 2 * BATCH * D0 * D1 + 2 * BATCH * D1 * D2
 
@@ -36,13 +44,19 @@ def tile_patchedsparsenetwork_pa_kernel(tc, x, W0, b0, m0, W1, b1, m1, out):
     with ExitStack() as ctx:
         ctx.enter_context(tc.manual_schedule())
         const = ctx.enter_context(tc.tile_pool(name="const", bufs=1))
-        weights = ctx.enter_context(tc.tile_pool(name="weights", bufs=AHEAD + 2))
-        stage = ctx.enter_context(tc.tile_pool(name="stage", bufs=3))
+        weights = ctx.enter_context(tc.tile_pool(name="weights", bufs=AHEAD + LAG_TRANSPOSE + 1))
+        grouped_pool = ctx.enter_context(
+            tc.tile_pool(name="grouped", bufs=LAG_QUANTISE - LAG_TRANSPOSE + 2)
+        )
+        codes_pool = ctx.enter_context(
+            tc.tile_pool(name="codes", bufs=LAG_MATMUL1 - LAG_QUANTISE + 2)
+        )
+        h_pool = ctx.enter_context(tc.tile_pool(name="h", bufs=2))
         tr_psum = ctx.enter_context(tc.psum_pool(name="tr_psum", bufs=4))
         acc_psum = ctx.enter_context(tc.psum_pool(name="acc_psum", bufs=4))
 
         w_of, m_of, grouped_of, codes_of, scales_of, acc_of = {}, {}, {}, {}, {}, {}
-        h_rows_of, result_of = {}, {}
+        h_rows_of = {}
 
         def load(i):
             w = weights.tile([P, UNIT], BF16, tag="w")
@@ -62,7 +76,7 @@ def tile_patchedsparsenetwork_pa_kernel(tc, x, W0, b0, m0, W1, b1, m1, out):
 
         def transpose(i):
             w_words = w_of[i][:].bitcast(F32)
-            grouped = stage.tile([P, UNIT], BF16, tag="grouped", align_bytes=64)
+            grouped = grouped_pool.tile([P, UNIT], BF16, tag="grouped", align_bytes=64)
             grouped_words = grouped[:].bitcast(F32).rearrange(
                 "p (a c q u) -> p a c q u", a=2, c=2, u=2
             )
@@ -77,8 +91,8 @@ def tile_patchedsparsenetwork_pa_kernel(tc, x, W0, b0, m0, W1, b1, m1, out):
             grouped_of[i] = grouped
 
         def quantise(i):
-            codes = stage.tile([P, UNIT // PACK], U32, tag="codes", align_bytes=64)
-            scales = stage.tile([P, UNIT // PACK], U8, tag="scales", align_bytes=64)
+            codes = codes_pool.tile([P, UNIT // PACK], U32, tag="codes", align_bytes=64)
+            scales = codes_pool.tile([P, UNIT // PACK], U8, tag="scales", align_bytes=64)
             nc.vector.quantize_mx(
                 out=codes[:].bitcast(FP8X4), scales=scales[:], in_=grouped_of[i][:]
             )
@@ -87,7 +101,7 @@ def tile_patchedsparsenetwork_pa_kernel(tc, x, W0, b0, m0, W1, b1, m1, out):
         def layer0_matmuls(j):
             g, u = divmod(j, 2)
             if u == 0:
-                h_rows = stage.tile([P, PACK, BATCH], BF16, tag="h_rows")
+                h_rows = h_pool.tile([P, PACK, BATCH], BF16, tag="h_rows")
                 h_rows_of[g] = h_rows
             for e in range(2):
                 acc = acc_psum.tile([P, BATCH], F32, tag="acc")
@@ -113,9 +127,10 @@ def tile_patchedsparsenetwork_pa_kernel(tc, x, W0, b0, m0, W1, b1, m1, out):
         def layer0_finish(j):
             g, u = divmod(j, 2)
             if u == 1:
-                h_grouped = stage.tile([P, BATCH, PACK], BF16, tag="h_grouped", align_bytes=64)
+                h_grouped = h_pool.tile([P, BATCH, PACK], BF16, tag="h_grouped", align_bytes=64)
                 nc.vector.tensor_copy(
-                    out=h_grouped[:], in_=h_rows_of[g][:].rearrange("p t n -> p n t")
+                    out=h_grouped[:].rearrange("p (c i) t -> p c t i", i=4),
+                    in_=h_rows_of[g][:].rearrange("p t (c i) -> p c t i", i=4),
                 )
                 h_cols = slice(BATCH * g, BATCH * (g + 1))
                 nc.vector.quantize_mx(
@@ -142,23 +157,20 @@ def tile_patchedsparsenetwork_pa_kernel(tc, x, W0, b0, m0, W1, b1, m1, out):
             acc_of[k] = acc
 
         def layer1_finish(k):
-            store, a = divmod(k, 2)
-            if a == 0:
-                result = stage.tile([P, BATCH_TILES, STORE_COLS], F32, tag="result")
-                result_of[store] = result
-            part = result_of[store][:, :, ROWS1 * a : ROWS1 * (a + 1)]
+            part = out_rows[:, :, ROWS1 * k : ROWS1 * (k + 1)]
             bias = b1_all[:, ROWS1 * k : ROWS1 * (k + 1)].unsqueeze(1)
             nc.vector.tensor_tensor(
                 out=part, in0=acc_of[k][:], in1=bias.to_broadcast([P, BATCH_TILES, ROWS1]), op=ADD
             )
             nc.scalar.activation(out=part, in_=part, func=RELU)
-            if a == 1:
-                cols = slice(STORE_COLS * store, STORE_COLS * (store + 1))
-                nc.scalar.dma_start(out=out_view[:, :, cols], in_=result_of[store][:])
+            if ROWS1 * (k + 1) % STORE_COLS == 0:
+                cols = slice(ROWS1 * (k + 1) - STORE_COLS, ROWS1 * (k + 1))
+                nc.sync.dma_start(out=out_view[:, :, cols], in_=out_rows[:, :, cols])
 
         x_rows = const.tile([P, BATCH_TILES * D0], BF16)
         nc.sync.dma_start(out=x_rows[:], in_=x.rearrange("(q r) k -> q (r k)", r=BATCH_TILES))
         out_view = out.rearrange("(q r) d -> q r d", r=BATCH_TILES)
+        out_rows = const.tile([P, BATCH_TILES, D2], F32)
 
         b0_rows = const.tile([P, 2 * P], BF16)
         b1_row = const.tile([P, D2], BF16)
@@ -206,20 +218,20 @@ def tile_patchedsparsenetwork_pa_kernel(tc, x, W0, b0, m0, W1, b1, m1, out):
         h_codes = const.tile([P, PASSES1 * BATCH], U32, align_bytes=64)
         h_scales = const.tile([P, PASSES1 * BATCH], U8, align_bytes=64)
 
-        for s in range(UNITS + 3):
+        for s in range(UNITS + LAG_FINISH1):
             if s + AHEAD < UNITS:
                 load(s + AHEAD)
-            if 0 <= s - 2 < UNITS:
-                quantise(s - 2)
-            if 0 <= s - 1 < UNITS:
-                transpose(s - 1)
-            if 0 <= s - 3 < UNITS0:
-                layer0_finish(s - 3)
-            if UNITS0 <= s - 3 < UNITS:
-                layer1_finish(s - 3 - UNITS0)
-            if 0 <= s - 2 < UNITS0:
-                layer0_matmuls(s - 2)
-            if UNITS0 <= s - 2 < UNITS:
-                layer1_matmuls(s - 2 - UNITS0)
+            if 0 <= s - LAG_QUANTISE < UNITS:
+                quantise(s - LAG_QUANTISE)
+            if 0 <= s - LAG_TRANSPOSE < UNITS:
+                transpose(s - LAG_TRANSPOSE)
+            if 0 <= s - LAG_FINISH0 < UNITS0:
+                layer0_finish(s - LAG_FINISH0)
+            if 0 <= s - LAG_FINISH1 - UNITS0 < UNITS1:
+                layer1_finish(s - LAG_FINISH1 - UNITS0)
+            if 0 <= s - LAG_MATMUL0 < UNITS0:
+                layer0_matmuls(s - LAG_MATMUL0)
+            if 0 <= s - LAG_MATMUL1 - UNITS0 < UNITS1:
+                layer1_matmuls(s - LAG_MATMUL1 - UNITS0)
             if s < UNITS:
                 multiply(s)

@@ -26,14 +26,13 @@ ROWS1 = P * UNIT // D1
 UNITS0 = D1 // ROWS0
 UNITS = UNITS0 + D2 // ROWS1
 UNITS1 = D2 // ROWS1
-STORE_COLS = 2 * ROWS1
 
 LAG_TRANSPOSE = 1
 LAG_QUANTISE = 3
 LAG_MATMUL0 = 3
 LAG_FINISH0 = 5
 LAG_MATMUL1 = 4
-LAG_FINISH1 = 6
+LAG_FINISH1 = 7
 AHEAD = 10
 
 FLOPS = 2 * BATCH * D0 * D1 + 2 * BATCH * D1 * D2
@@ -163,9 +162,7 @@ def tile_patchedsparsenetwork_pa_kernel(tc, x, W0, b0, m0, W1, b1, m1, out):
                 out=part, in0=acc_of[k][:], in1=bias.to_broadcast([P, BATCH_TILES, ROWS1]), op=ADD
             )
             nc.scalar.activation(out=part, in_=part, func=RELU)
-            if ROWS1 * (k + 1) % STORE_COLS == 0:
-                cols = slice(ROWS1 * (k + 1) - STORE_COLS, ROWS1 * (k + 1))
-                nc.sync.dma_start(out=out_view[:, :, cols], in_=out_rows[:, :, cols])
+            nc.sync.dma_start(out=out_view[:, :, ROWS1 * k : ROWS1 * (k + 1)], in_=part)
 
         x_rows = const.tile([P, BATCH_TILES * D0], BF16)
         nc.sync.dma_start(out=x_rows[:], in_=x.rearrange("(q r) k -> q (r k)", r=BATCH_TILES))

from contextlib import ExitStack

import concourse.mybir as mybir
from concourse.masks import make_identity

F32 = mybir.dt.float32
BF16 = mybir.dt.bfloat16
U32 = mybir.dt.uint32
U8 = mybir.dt.uint8
FP8X4 = mybir.dt.float8_e4m3fn_x4
MULT = mybir.AluOpType.mult
ADD = mybir.AluOpType.add
RELU = mybir.ActivationFunctionType.Relu

P = 128
PACK = 4
K_PASS = P * PACK
BANK = 512
BATCH, D0, D1, D2 = 512, 1024, 2048, 2048
PASSES0 = D0 // K_PASS
PASSES1 = D1 // K_PASS
BATCH_TILES = BATCH // P
UNIT = 2048
ROWS0 = P * UNIT // D0
ROWS1 = P * UNIT // D1
UNITS0 = D1 // ROWS0
UNITS = UNITS0 + D2 // ROWS1
UNITS1 = D2 // ROWS1

LAG_TRANSPOSE = 1
LAG_QUANTISE = 3
LAG_MATMUL0 = 3
LAG_FINISH0 = 5
LAG_MATMUL1 = 4
LAG_FINISH1 = 7
AHEAD = 10

FLOPS = 2 * BATCH * D0 * D1 + 2 * BATCH * D1 * D2


def tile_patchedsparsenetwork_pa_kernel(tc, x, W0, b0, m0, W1, b1, m1, out):
    nc = tc.nc
    with ExitStack() as ctx:
        ctx.enter_context(tc.manual_schedule())
        const = ctx.enter_context(tc.tile_pool(name="const", bufs=1))
        weights = ctx.enter_context(tc.tile_pool(name="weights", bufs=AHEAD + LAG_TRANSPOSE + 1))
        grouped_pool = ctx.enter_context(
            tc.tile_pool(name="grouped", bufs=LAG_QUANTISE - LAG_TRANSPOSE + 2)
        )
        codes_pool = ctx.enter_context(
            tc.tile_pool(name="codes", bufs=LAG_MATMUL1 - LAG_QUANTISE + 2)
        )
        h_pool = ctx.enter_context(tc.tile_pool(name="h", bufs=2))
        tr_psum = ctx.enter_context(tc.psum_pool(name="tr_psum", bufs=4))
        acc_psum = ctx.enter_context(tc.psum_pool(name="acc_psum", bufs=4))

        w_of, m_of, grouped_of, codes_of, scales_of, acc_of = {}, {}, {}, {}, {}, {}
        h_rows_of = {}

        def load(i):
            w = weights.tile([P, UNIT], BF16, tag="w")
            m = weights.tile([P, UNIT], BF16, tag="m")
            if i < UNITS0:
                rows = slice(ROWS0 * i, ROWS0 * (i + 1))
                nc.sync.dma_start(out=w[:], in_=W0[rows, :].rearrange("(q e) k -> q (e k)", e=2))
                nc.sync.dma_start(out=m[:], in_=m0[rows, :].rearrange("(q e) k -> q (e k)", e=2))
            else:
                rows = slice(ROWS1 * (i - UNITS0), ROWS1 * (i - UNITS0 + 1))
                nc.sync.dma_start(out=w[:], in_=W1[rows, :])
                nc.sync.dma_start(out=m[:], in_=m1[rows, :])
            w_of[i], m_of[i] = w, m

        def multiply(i):
            nc.vector.tensor_tensor(out=w_of[i][:], in0=w_of[i][:], in1=m_of[i][:], op=MULT)

        def transpose(i):
            w_words = w_of[i][:].bitcast(F32)
            grouped = grouped_pool.tile([P, UNIT], BF16, tag="grouped", align_bytes=64)
            grouped_words = grouped[:].bitcast(F32).rearrange(
                "p (a c q u) -> p a c q u", a=2, c=2, u=2
            )
            for a in range(2):
                bank = tr_psum.tile([P, 4, P], F32, tag="tr")
                for s in range(4):
                    first = P * (4 * a + s)
                    nc.tensor.transpose(bank[:, s, :], w_words[:, first : first + P], ident[:])
                nc.scalar.copy(
                    out=grouped_words[:, a], in_=bank[:].rearrange("p (c u) q -> p c q u", u=2)
                )
            grouped_of[i] = grouped

        def quantise(i):
            codes = codes_pool.tile([P, UNIT // PACK], U32, tag="codes", align_bytes=64)
            scales = codes_pool.tile([P, UNIT // PACK], U8, tag="scales", align_bytes=64)
            nc.vector.quantize_mx(
                out=codes[:].bitcast(FP8X4), scales=scales[:], in_=grouped_of[i][:]
            )
            codes_of[i], scales_of[i] = codes, scales

        def layer0_matmuls(j):
            g, u = divmod(j, 2)
            if u == 0:
                h_rows = h_pool.tile([P, PACK, BATCH], BF16, tag="h_rows")
                h_rows_of[g] = h_rows
            for e in range(2):
                acc = acc_psum.tile([P, BATCH], F32, tag="acc")
                for g0 in range(PASSES0):
                    w_cols = slice(P * (PASSES0 * e + g0), P * (PASSES0 * e + g0 + 1))
                    x_cols = slice(BATCH * g0, BATCH * (g0 + 1))
                    nc.tensor.matmul_mx(
                        out=acc[:],
                        lhsT=codes_of[j][:, w_cols].bitcast(FP8X4),
                        lhsT_scale=scales_of[j][:, w_cols],
                        rhs=x_codes[:, x_cols].bitcast(FP8X4),
                        rhs_scale=x_scales[:, x_cols],
                        start=(g0 == 0),
                        stop=(g0 == PASSES0 - 1),
                    )
                nc.scalar.activation(
                    out=h_rows_of[g][:, 2 * u + e, :],
                    in_=acc[:],
                    func=RELU,
                    bias=b0_cols[:, 2 * j + e : 2 * j + e + 1],
                )

        def layer0_finish(j):
            g, u = divmod(j, 2)
            if u == 1:
                h_grouped = h_pool.tile([P, BATCH, PACK], BF16, tag="h_grouped", align_bytes=64)
                nc.vector.tensor_copy(
                    out=h_grouped[:].rearrange("p (c i) t -> p c t i", i=4),
                    in_=h_rows_of[g][:].rearrange("p t (c i) -> p c t i", i=4),
                )
                h_cols = slice(BATCH * g, BATCH * (g + 1))
                nc.vector.quantize_mx(
                    out=h_codes[:, h_cols].bitcast(FP8X4),
                    scales=h_scales[:, h_cols],
                    in_=h_grouped[:].rearrange("p n t -> p (n t)"),
                )

        def layer1_matmuls(k):
            acc = acc_psum.tile([P, BATCH_TILES, ROWS1], F32, tag="acc")
            for r in range(BATCH_TILES):
                for g in range(PASSES1):
                    h_cols = slice(BATCH * g + P * r, BATCH * g + P * (r + 1))
                    w_cols = slice(ROWS1 * g, ROWS1 * (g + 1))
                    nc.tensor.matmul_mx(
                        out=acc[:, r, :],
                        lhsT=h_codes[:, h_cols].bitcast(FP8X4),
                        lhsT_scale=h_scales[:, h_cols],
                        rhs=codes_of[UNITS0 + k][:, w_cols].bitcast(FP8X4),
                        rhs_scale=scales_of[UNITS0 + k][:, w_cols],
                        start=(g == 0),
                        stop=(g == PASSES1 - 1),
                    )
            acc_of[k] = acc

        def layer1_finish(k):
            part = out_rows[:, :, ROWS1 * k : ROWS1 * (k + 1)]
            bias = b1_all[:, ROWS1 * k : ROWS1 * (k + 1)].unsqueeze(1)
            nc.vector.tensor_tensor(
                out=part, in0=acc_of[k][:], in1=bias.to_broadcast([P, BATCH_TILES, ROWS1]), op=ADD
            )
            nc.scalar.activation(out=part, in_=part, func=RELU)
            nc.sync.dma_start(out=out_view[:, :, ROWS1 * k : ROWS1 * (k + 1)], in_=part)

        x_rows = const.tile([P, BATCH_TILES * D0], BF16)
        nc.sync.dma_start(out=x_rows[:], in_=x.rearrange("(q r) k -> q (r k)", r=BATCH_TILES))
        out_view = out.rearrange("(q r) d -> q r d", r=BATCH_TILES)
        out_rows = const.tile([P, BATCH_TILES, D2], F32)

        b0_rows = const.tile([P, 2 * P], BF16)
        b1_row = const.tile([P, D2], BF16)
        ones = const.tile([P, P], BF16)
        nc.vector.memset(b0_rows[:], 0.0)
        nc.vector.memset(b1_row[:], 0.0)
        nc.vector.memset(ones[:], 1.0)
        nc.sync.dma_start(out=b0_rows[0 : D1 // 256, :], in_=b0.rearrange("(j c) -> j c", c=256))
        nc.sync.dma_start(out=b1_row[0:1, :], in_=b1.rearrange("(o d) -> o d", o=1))
        for i in range(AHEAD):
            load(i)

        ident = const.tile([P, P], F32)
        make_identity(nc, ident[:])

        x_words = x_rows[:].bitcast(F32).rearrange("q (r w) -> q r w", r=BATCH_TILES)
        x_grouped = const.tile([P, PASSES0 * BATCH * PACK], BF16, align_bytes=64)
        x_grouped_words = x_grouped[:].bitcast(F32).rearrange(
            "p (g r q u) -> p g r q u", g=PASSES0, r=BATCH_TILES, u=2
        )
        for r in range(BATCH_TILES):
            bank = tr_psum.tile([P, 4, P], F32, tag="tr")
            for s in range(4):
                nc.tensor.transpose(bank[:, s, :], x_words[:, r, P * s : P * (s + 1)], ident[:])
            nc.scalar.copy(
                out=x_grouped_words[:, :, r, :, :],
                in_=bank[:].rearrange("p (g u) q -> p g q u", u=2),
            )
        x_codes = const.tile([P, PASSES0 * BATCH], U32, align_bytes=64)
        x_scales = const.tile([P, PASSES0 * BATCH], U8, align_bytes=64)
        nc.vector.quantize_mx(out=x_codes[:].bitcast(FP8X4), scales=x_scales[:], in_=x_grouped[:])

        b0_bank = tr_psum.tile([P, BANK], F32, tag="tr")
        nc.tensor.transpose(b0_bank[:, 0:P], b0_rows[:].bitcast(F32), ident[:])
        b0_cols = const.tile([P, D1 // P], F32)
        nc.vector.tensor_copy(out=b0_cols[:], in_=b0_bank[:, 0 : D1 // 256].bitcast(BF16))

        b1_all = const.tile([P, D2], F32)
        for i in range(D2 // BANK):
            cols = slice(BANK * i, BANK * (i + 1))
            b1_bank = acc_psum.tile([P, BANK], F32, tag="acc")
            nc.tensor.matmul(b1_bank[:], lhsT=ones[:], rhs=b1_row[:, cols], start=True, stop=True)
            nc.scalar.copy(out=b1_all[:, cols], in_=b1_bank[:])

        h_codes = const.tile([P, PASSES1 * BATCH], U32, align_bytes=64)
        h_scales = const.tile([P, PASSES1 * BATCH], U8, align_bytes=64)

        for s in range(UNITS + LAG_FINISH1):
            if s + AHEAD < UNITS:
                load(s + AHEAD)
            if 0 <= s - LAG_QUANTISE < UNITS:
                quantise(s - LAG_QUANTISE)
            if 0 <= s - LAG_TRANSPOSE < UNITS:
                transpose(s - LAG_TRANSPOSE)
            if 0 <= s - LAG_FINISH0 < UNITS0:
                layer0_finish(s - LAG_FINISH0)
            if 0 <= s - LAG_FINISH1 - UNITS0 < UNITS1:
                layer1_finish(s - LAG_FINISH1 - UNITS0)
            if 0 <= s - LAG_MATMUL0 < UNITS0:
                layer0_matmuls(s - LAG_MATMUL0)
            if 0 <= s - LAG_MATMUL1 - UNITS0 < UNITS1:
                layer1_matmuls(s - LAG_MATMUL1 - UNITS0)
            if s < UNITS:
                multiply(s)
